import numpy as np
import ml_dtypes


def mxq(x, axis, fmt="e4m3"):
    dtype, down = {"e4m3": (ml_dtypes.float8_e4m3fn, 7), "e5m2": (ml_dtypes.float8_e5m2, 14)}[fmt]
    v = np.moveaxis(np.asarray(x, np.float32).astype(ml_dtypes.bfloat16).astype(np.float64), axis, -1)
    blocks = v.reshape(v.shape[:-1] + (-1, 32))
    amax = np.abs(blocks).max(-1, keepdims=True)
    byte = np.maximum(np.where(amax > 0, np.frexp(amax)[1] - 1 + 127, 0) - down, 1)
    scale = np.exp2(byte - 127.0)
    codes = (blocks / scale).astype(np.float32).astype(dtype).astype(np.float64)
    return np.moveaxis((codes * scale).reshape(v.shape), -1, axis)


WIDE = False


def mx_kscale(k):
    if not WIDE:
        return np.ones(k)
    levels = np.array([10, -10, 5, -5, 0])
    a = np.random.permutation(np.resize(levels, k // 512 * 4)).reshape(k // 512, 4)
    idx = np.arange(k)
    return np.exp2(a[idx // 512, idx % 128 // 32])


BF16 = ml_dtypes.bfloat16


def bf(x):
    return np.asarray(x, np.float32).astype(BF16)


def f64(x):
    return np.asarray(x).astype(np.float64)


B, S, DIM, H, NOPE, ROPE, VD = 4, 128, 2048, 16, 128, 64, 128
QK = NOPE + ROPE


def apply_rope(t, freqs):
    b, s, h, d = t.shape
    tr = t.reshape(b, s, h, d // 2, 2)
    cos = np.cos(freqs)[None, :, None, :]
    sin = np.sin(freqs)[None, :, None, :]
    out = np.stack([tr[..., 0] * cos - tr[..., 1] * sin,
                    tr[..., 0] * sin + tr[..., 1] * cos], axis=-1)
    return out.reshape(b, s, h, d)


def setup_inputs():
    s = mx_kscale(DIM)
    inv_freq = 1.0 / (10000.0 ** (np.arange(0, ROPE, 2) / ROPE))
    ang = np.arange(S)[:, None] * inv_freq[None, :]
    ang = ang - 2.0 * np.pi * np.round(ang / (2.0 * np.pi))
    return {"x": bf(np.random.standard_normal((B, S, DIM)) * s),
            "w": bf(np.random.standard_normal((DIM, H * QK)) / np.sqrt(DIM) / s[:, None]),
            "freqs": bf(ang)}


def reference(x, w, freqs):
    y = mxq(f64(x), 2, "e4m3") @ mxq(f64(w), 0, "e4m3")
    nope = y[..., :H * NOPE].reshape(B, S, H, NOPE)
    rope = apply_rope(y[..., H * NOPE:].reshape(B, S, H, ROPE), f64(freqs))
    return np.concatenate([nope, rope], axis=-1)

@@ -1,0 +1,154 @@
+import concourse.mybir as mybir
+from concourse.masks import make_identity
+
+BF16 = mybir.dt.bfloat16
+F32 = mybir.dt.float32
+U32 = mybir.dt.uint32
+U8 = mybir.dt.uint8
+FP8X4 = mybir.dt.float8_e4m3fn_x4
+ACT = mybir.ActivationFunctionType
+ALU = mybir.AluOpType
+
+P = 128
+PACK = 4
+K_PASS = P * PACK
+BATCH = 4
+DIM = 2048
+HEADS = 16
+NOPE = 128
+ROPE = 64
+QK = NOPE + ROPE
+PAIRS = ROPE // 2
+PASSES = DIM // K_PASS
+BANK = 512
+ROUND = 2 * BANK
+PIECE = 256
+FLOPS = 2 * BATCH * P * DIM * HEADS * QK
+
+
+def tile_mla_pa_kernel(tc, x, w, freqs, out):
+    nc = tc.nc
+    with tc.tile_pool(name="const", bufs=1) as const, tc.tile_pool(name="keep", bufs=1) as keep, tc.tile_pool(
+        name="x_in", bufs=4
+    ) as x_in, tc.tile_pool(name="x_side", bufs=2) as x_side, tc.tile_pool(name="w_in", bufs=10) as w_in, tc.tile_pool(
+        name="w_side", bufs=7
+    ) as w_side, tc.tile_pool(name="w_mx", bufs=8) as w_mx, tc.tile_pool(name="turn", bufs=3) as turn, tc.psum_pool(
+        name="psum", bufs=8
+    ) as psum:
+        ident = const.tile([P, P], F32)
+        make_identity(nc, ident[:])
+        x_codes = keep.tile([P, BATCH, PASSES * P], U32, align_bytes=64)
+        x_scales = keep.tile([P, BATCH, PASSES * P], U8, align_bytes=64)
+        for b in range(BATCH):
+            x_rows = x_in.tile([P, DIM], BF16)
+            nc.sync.dma_start(out=x_rows[:], in_=x[b])
+            x_words = x_rows[:].bitcast(F32).rearrange("s (g q u) -> s g u q", g=PASSES, u=2)
+            x_grouped = x_side.tile([P, PASSES * P * PACK], BF16, align_bytes=64)
+            grouped_words = x_grouped[:].bitcast(F32).rearrange("q (g s u) -> q g s u", g=PASSES, u=2)
+            for first in range(0, PASSES, 2):
+                flipped = psum.tile([P, 2, 2, P], F32, tag="bank")
+                for i in range(2):
+                    for u in range(2):
+                        nc.tensor.transpose(flipped[:, i, u, :], x_words[:, first + i, u, :], ident[:])
+                nc.scalar.copy(
+                    out=grouped_words[:, first : first + 2, :, :], in_=flipped[:].rearrange("q g u s -> q g s u")
+                )
+            nc.vector.quantize_mx(out=x_codes[:, b, :].bitcast(FP8X4), scales=x_scales[:, b, :], in_=x_grouped[:])
+
+        angles = const.tile([P, PAIRS], BF16)
+        nc.sync.dma_start(out=angles[:], in_=freqs)
+        sines = const.tile([P, 2, PAIRS], F32)
+        nc.scalar.activation(out=sines[:, 0, :], in_=angles[:], func=ACT.Sin, scale=-1.0)
+        nc.scalar.activation(out=sines[:, 1, :], in_=angles[:], func=ACT.Sin)
+        sin_half = const.tile([P, PAIRS], F32)
+        nc.scalar.activation(out=sin_half[:], in_=angles[:], func=ACT.Sin, scale=0.5)
+        sin_half_sq = const.tile([P, PAIRS], F32)
+        nc.vector.tensor_tensor(out=sin_half_sq[:], in0=sin_half[:], in1=sin_half[:], op=ALU.mult)
+        cosines = const.tile([P, PAIRS, 2], F32)
+        nc.vector.tensor_scalar(
+            out=cosines[:],
+            in0=sin_half_sq[:].unsqueeze(2).to_broadcast([P, PAIRS, 2]),
+            scalar1=-2.0,
+            scalar2=1.0,
+            op0=ALU.mult,
+            op1=ALU.add,
+        )
+
+        result = [keep.tile([P, HEADS, QK], F32, name="result%d" % b) for b in range(BATCH)]
+
+        def rotate(bank, b, head0):
+            heads = BANK // ROPE
+            rotary = result[b][:, head0 : head0 + heads, NOPE:QK]
+            pairs = bank[:].rearrange("s (h j e) -> s h j e", j=PAIRS, e=2)
+            nc.vector.tensor_tensor(
+                out=rotary,
+                in0=bank[:].rearrange("s (h c) -> s h c", c=ROPE),
+                in1=cosines[:].rearrange("s j e -> s (j e)").unsqueeze(1).to_broadcast([P, heads, ROPE]),
+                op=ALU.mult,
+            )
+            crossed = turn.tile([P, 2, heads, PAIRS], F32)
+            for e in range(2):
+                nc.vector.tensor_tensor(
+                    out=crossed[:, e, :, :],
+                    in0=pairs[:, :, :, 1 - e],
+                    in1=sines[:, e, :].unsqueeze(1).to_broadcast([P, heads, PAIRS]),
+                    op=ALU.mult,
+                )
+            nc.vector.tensor_tensor(
+                out=rotary.rearrange("s h (j e) -> s h j e", e=2),
+                in0=rotary.rearrange("s h (j e) -> s h j e", e=2),
+                in1=crossed[:].rearrange("s e h j -> s h j e"),
+                op=ALU.add,
+            )
+
+        for col0 in (HEADS * NOPE, 0, ROUND):
+            banks = [
+                [psum.tile([P, BANK], F32, tag="bank", name="bank%d%d" % (b, half)) for half in range(2)]
+                for b in range(BATCH)
+            ]
+            for g in range(PASSES):
+                w_rows = w_in.tile([P, PACK, ROUND], BF16)
+                nc.sync.dma_start(
+                    out=w_rows[:],
+                    in_=w[g * K_PASS : (g + 1) * K_PASS, col0 : col0 + ROUND].rearrange("(p j) n -> p j n", j=PACK),
+                )
+                for half in range(2):
+                    w_grouped = w_side.tile([P, BANK, PACK], BF16, align_bytes=64)
+                    for n0 in range(0, BANK, PIECE):
+                        nc.any.tensor_copy(
+                            out=w_grouped[:, n0 : n0 + PIECE, :].rearrange("p (c i) j -> p c j i", i=4),
+                            in_=w_rows[:, :, half * BANK + n0 : half * BANK + n0 + PIECE].rearrange(
+                                "p j (c i) -> p c j i", i=4
+                            ),
+                        )
+                    w_codes = w_mx.tile([P, BANK], U32, align_bytes=64)
+                    w_scales = w_mx.tile([P, BANK], U8, align_bytes=64)
+                    nc.vector.quantize_mx(
+                        out=w_codes[:].bitcast(FP8X4),
+                        scales=w_scales[:],
+                        in_=w_grouped[:].rearrange("p n j -> p (n j)"),
+                    )
+                    for b in range(BATCH):
+                        nc.tensor.matmul_mx(
+                            out=banks[b][half][:],
+                            lhsT=x_codes[:, b, g * P : (g + 1) * P].bitcast(FP8X4),
+                            lhsT_scale=x_scales[:, b, g * P : (g + 1) * P],
+                            rhs=w_codes[:].bitcast(FP8X4),
+                            rhs_scale=w_scales[:],
+                            start=(g == 0),
+                            stop=(g == PASSES - 1),
+                        )
+            for half in range(2):
+                for b in range(BATCH):
+                    if col0 == HEADS * NOPE:
+                        rotate(banks[b][half], b, half * (BANK // ROPE))
+                    else:
+                        heads = BANK // NOPE
+                        head0 = (col0 + half * BANK) // NOPE
+                        nc.any.tensor_copy(
+                            out=result[b][:, head0 : head0 + heads, 0:NOPE],
+                            in_=banks[b][half][:].rearrange("s (h c) -> s h c", c=NOPE),
+                        )
+                        nc.sync.dma_start(
+                            out=out[b, :, head0 : head0 + heads, :], in_=result[b][:, head0 : head0 + heads, :]
+                        )

@@ -21,28 +21,62 @@ QK = NOPE + ROPE
 PAIRS = ROPE // 2
 PASSES = DIM // K_PASS
 BANK = 512
-ROUND = 2 * BANK
-PIECE = 256
+ROTARY_COL0 = HEADS * NOPE
+ROTARY_ROUNDS = HEADS * ROPE // BANK
+ROUNDS = HEADS * QK // BANK
+UNITS = ROUNDS * PASSES
+ROTARY_BANKS = ROTARY_ROUNDS * BATCH
+VECTOR_COLS = 320
 FLOPS = 2 * BATCH * P * DIM * HEADS * QK
 
 
 def tile_mla_pa_kernel(tc, x, w, freqs, out):
     nc = tc.nc
     with tc.tile_pool(name="const", bufs=1) as const, tc.tile_pool(name="keep", bufs=1) as keep, tc.tile_pool(
-        name="x_in", bufs=4
-    ) as x_in, tc.tile_pool(name="x_side", bufs=2) as x_side, tc.tile_pool(name="w_in", bufs=10) as w_in, tc.tile_pool(
-        name="w_side", bufs=7
-    ) as w_side, tc.tile_pool(name="w_mx", bufs=8) as w_mx, tc.tile_pool(name="turn", bufs=3) as turn, tc.psum_pool(
+        name="x_in", bufs=BATCH
+    ) as x_in, tc.tile_pool(name="x_side", bufs=2) as x_side, tc.tile_pool(
+        name="w_narrow", bufs=ROTARY_ROUNDS * PASSES
+    ) as w_narrow, tc.tile_pool(name="w_wide", bufs=2 * PASSES) as w_wide, tc.tile_pool(
+        name="w_side", bufs=4
+    ) as w_side, tc.tile_pool(name="w_mx", bufs=4) as w_mx, tc.tile_pool(name="turn", bufs=3) as turn, tc.psum_pool(
         name="psum", bufs=8
-    ) as psum:
+    ) as psum, tc.manual_schedule():
+        angles = const.tile([P, PAIRS], BF16)
+        nc.scalar.dma_start(out=angles[:], in_=freqs)
+        x_rows = []
+        for b in range(BATCH):
+            rows = x_in.tile([P, DIM], BF16, name="x_rows")
+            nc.sync.dma_start(out=rows[:], in_=x[b])
+            x_rows.append(rows)
+
+        def load_w(pool, col0, width, g):
+            rows = pool.tile([P, PACK, width], BF16, name="w_rows")
+            nc.sync.dma_start(
+                out=rows[:],
+                in_=w[g * K_PASS : (g + 1) * K_PASS, col0 : col0 + width].rearrange("(p j) n -> p j n", j=PACK),
+            )
+            return rows
+
+        w_rows = []
+        for r in range(ROTARY_ROUNDS):
+            w_rows.append([load_w(w_narrow, ROTARY_COL0 + r * BANK, BANK, g)[:] for g in range(PASSES)])
+        for col0 in range(0, ROTARY_COL0, 2 * BANK):
+            wide = [load_w(w_wide, col0, 2 * BANK, g) for g in range(PASSES)]
+            for half in range(2):
+                w_rows.append([rows[:, :, half * BANK : (half + 1) * BANK] for rows in wide])
+
+        sines = const.tile([P, 2, PAIRS], F32)
+        nc.scalar.activation(out=sines[:, 0, :], in_=angles[:], func=ACT.Sin, scale=-1.0)
+        nc.scalar.activation(out=sines[:, 1, :], in_=angles[:], func=ACT.Sin)
+        sin_half = const.tile([P, PAIRS], F32)
+        nc.scalar.activation(out=sin_half[:], in_=angles[:], func=ACT.Sin, scale=0.5)
+
         ident = const.tile([P, P], F32)
         make_identity(nc, ident[:])
         x_codes = keep.tile([P, BATCH, PASSES * P], U32, align_bytes=64)
         x_scales = keep.tile([P, BATCH, PASSES * P], U8, align_bytes=64)
         for b in range(BATCH):
-            x_rows = x_in.tile([P, DIM], BF16)
-            nc.sync.dma_start(out=x_rows[:], in_=x[b])
-            x_words = x_rows[:].bitcast(F32).rearrange("s (g q u) -> s g u q", g=PASSES, u=2)
+            x_words = x_rows[b][:].bitcast(F32).rearrange("s (g q u) -> s g u q", g=PASSES, u=2)
             x_grouped = x_side.tile([P, PASSES * P * PACK], BF16, align_bytes=64)
             grouped_words = x_grouped[:].bitcast(F32).rearrange("q (g s u) -> q g s u", g=PASSES, u=2)
             for first in range(0, PASSES, 2):
@@ -55,13 +89,6 @@ def tile_mla_pa_kernel(tc, x, w, freqs, out):
                 )
             nc.vector.quantize_mx(out=x_codes[:, b, :].bitcast(FP8X4), scales=x_scales[:, b, :], in_=x_grouped[:])
 
-        angles = const.tile([P, PAIRS], BF16)
-        nc.sync.dma_start(out=angles[:], in_=freqs)
-        sines = const.tile([P, 2, PAIRS], F32)
-        nc.scalar.activation(out=sines[:, 0, :], in_=angles[:], func=ACT.Sin, scale=-1.0)
-        nc.scalar.activation(out=sines[:, 1, :], in_=angles[:], func=ACT.Sin)
-        sin_half = const.tile([P, PAIRS], F32)
-        nc.scalar.activation(out=sin_half[:], in_=angles[:], func=ACT.Sin, scale=0.5)
         sin_half_sq = const.tile([P, PAIRS], F32)
         nc.vector.tensor_tensor(out=sin_half_sq[:], in0=sin_half[:], in1=sin_half[:], op=ALU.mult)
         cosines = const.tile([P, PAIRS, 2], F32)
@@ -76,16 +103,49 @@ def tile_mla_pa_kernel(tc, x, w, freqs, out):
 
         result = [keep.tile([P, HEADS, QK], F32, name="result%d" % b) for b in range(BATCH)]
 
-        def rotate(bank, b, head0):
+        def regroup(unit, vector_cols):
+            rows = w_rows[unit // PASSES][unit % PASSES]
+            w_grouped = w_side.tile([P, BANK, PACK], BF16, align_bytes=64)
+            for copy, lo, hi in ((nc.vector.tensor_copy, 0, vector_cols), (nc.scalar.copy, vector_cols, BANK)):
+                if lo < hi:
+                    copy(
+                        out=w_grouped[:, lo:hi, :].rearrange("p (c i) j -> p c j i", i=4),
+                        in_=rows[:, :, lo:hi].rearrange("p j (c i) -> p c j i", i=4),
+                    )
+            return w_grouped
+
+        def multiply(unit, w_grouped, banks):
+            g = unit % PASSES
+            w_codes = w_mx.tile([P, BANK], U32, align_bytes=64)
+            w_scales = w_mx.tile([P, BANK], U8, align_bytes=64)
+            nc.vector.quantize_mx(
+                out=w_codes[:].bitcast(FP8X4), scales=w_scales[:], in_=w_grouped[:].rearrange("p n j -> p (n j)")
+            )
+            for b in range(BATCH):
+                nc.tensor.matmul_mx(
+                    out=banks[b][:],
+                    lhsT=x_codes[:, b, g * P : (g + 1) * P].bitcast(FP8X4),
+                    lhsT_scale=x_scales[:, b, g * P : (g + 1) * P],
+                    rhs=w_codes[:].bitcast(FP8X4),
+                    rhs_scale=w_scales[:],
+                    start=(g == 0),
+                    stop=(g == PASSES - 1),
+                )
+
+        def rotary_part(n):
             heads = BANK // ROPE
-            rotary = result[b][:, head0 : head0 + heads, NOPE:QK]
-            pairs = bank[:].rearrange("s (h j e) -> s h j e", j=PAIRS, e=2)
+            head0 = (n // BATCH) * heads
+            return result[n % BATCH][:, head0 : head0 + heads, NOPE:QK]
+
+        def rotation_products(n, bank):
+            heads = BANK // ROPE
             nc.vector.tensor_tensor(
-                out=rotary,
+                out=rotary_part(n),
                 in0=bank[:].rearrange("s (h c) -> s h c", c=ROPE),
                 in1=cosines[:].rearrange("s j e -> s (j e)").unsqueeze(1).to_broadcast([P, heads, ROPE]),
                 op=ALU.mult,
             )
+            pairs = bank[:].rearrange("s (h j e) -> s h j e", j=PAIRS, e=2)
             crossed = turn.tile([P, 2, heads, PAIRS], F32)
             for e in range(2):
                 nc.vector.tensor_tensor(
@@ -94,61 +154,37 @@ def tile_mla_pa_kernel(tc, x, w, freqs, out):
                     in1=sines[:, e, :].unsqueeze(1).to_broadcast([P, heads, PAIRS]),
                     op=ALU.mult,
                 )
-            nc.vector.tensor_tensor(
-                out=rotary.rearrange("s h (j e) -> s h j e", e=2),
-                in0=rotary.rearrange("s h (j e) -> s h j e", e=2),
-                in1=crossed[:].rearrange("s e h j -> s h j e"),
-                op=ALU.add,
-            )
+            return crossed
 
-        for col0 in (HEADS * NOPE, 0, ROUND):
-            banks = [
-                [psum.tile([P, BANK], F32, tag="bank", name="bank%d%d" % (b, half)) for half in range(2)]
-                for b in range(BATCH)
-            ]
-            for g in range(PASSES):
-                w_rows = w_in.tile([P, PACK, ROUND], BF16)
-                nc.sync.dma_start(
-                    out=w_rows[:],
-                    in_=w[g * K_PASS : (g + 1) * K_PASS, col0 : col0 + ROUND].rearrange("(p j) n -> p j n", j=PACK),
+        def rotation_sum(n, crossed):
+            pairs = rotary_part(n).rearrange("s h (j e) -> s h j e", e=2)
+            nc.vector.tensor_tensor(out=pairs, in0=pairs, in1=crossed[:].rearrange("s e h j -> s h j e"), op=ALU.add)
+
+        def store_plain(n, bank, copy):
+            heads = BANK // NOPE
+            head0 = (n // BATCH) * heads
+            b = n % BATCH
+            copy(out=result[b][:, head0 : head0 + heads, 0:NOPE], in_=bank[:].rearrange("s (h c) -> s h c", c=NOPE))
+            nc.sync.dma_start(out=out[b, :, head0 : head0 + heads, :], in_=result[b][:, head0 : head0 + heads, :])
+
+        banks = []
+        side_tiles = []
+        regrouped = [regroup(0, VECTOR_COLS)]
+        for step in range(UNITS + BATCH):
+            emptied = step - PASSES
+            rotating = 0 <= emptied < ROTARY_BANKS
+            if step + 1 < UNITS:
+                regrouped.append(regroup(step + 1, 0 if rotating else VECTOR_COLS))
+            if step < UNITS:
+                if step % PASSES == 0:
+                    banks.extend(psum.tile([P, BANK], F32, tag="bank", name="bank%d" % b) for b in range(BATCH))
+                multiply(step, regrouped[step], banks[-BATCH:])
+            if rotating:
+                side_tiles.append(rotation_products(emptied, banks[emptied]))
+            if 0 <= emptied - 1 < ROTARY_BANKS:
+                rotation_sum(emptied - 1, side_tiles[emptied - 1])
+            if emptied >= ROTARY_BANKS:
+                idle_vector = step >= UNITS and emptied % 2 == 1
+                store_plain(
+                    emptied - ROTARY_BANKS, banks[emptied], nc.vector.tensor_copy if idle_vector else nc.scalar.copy
                 )
-                for half in range(2):
-                    w_grouped = w_side.tile([P, BANK, PACK], BF16, align_bytes=64)
-                    for n0 in range(0, BANK, PIECE):
-                        nc.any.tensor_copy(
-                            out=w_grouped[:, n0 : n0 + PIECE, :].rearrange("p (c i) j -> p c j i", i=4),
-                            in_=w_rows[:, :, half * BANK + n0 : half * BANK + n0 + PIECE].rearrange(
-                                "p j (c i) -> p c j i", i=4
-                            ),
-                        )
-                    w_codes = w_mx.tile([P, BANK], U32, align_bytes=64)
-                    w_scales = w_mx.tile([P, BANK], U8, align_bytes=64)
-                    nc.vector.quantize_mx(
-                        out=w_codes[:].bitcast(FP8X4),
-                        scales=w_scales[:],
-                        in_=w_grouped[:].rearrange("p n j -> p (n j)"),
-                    )
-                    for b in range(BATCH):
-                        nc.tensor.matmul_mx(
-                            out=banks[b][half][:],
-                            lhsT=x_codes[:, b, g * P : (g + 1) * P].bitcast(FP8X4),
-                            lhsT_scale=x_scales[:, b, g * P : (g + 1) * P],
-                            rhs=w_codes[:].bitcast(FP8X4),
-                            rhs_scale=w_scales[:],
-                            start=(g == 0),
-                            stop=(g == PASSES - 1),
-                        )
-            for half in range(2):
-                for b in range(BATCH):
-                    if col0 == HEADS * NOPE:
-                        rotate(banks[b][half], b, half * (BANK // ROPE))
-                    else:
-                        heads = BANK // NOPE
-                        head0 = (col0 + half * BANK) // NOPE
-                        nc.any.tensor_copy(
-                            out=result[b][:, head0 : head0 + heads, 0:NOPE],
-                            in_=banks[b][half][:].rearrange("s (h c) -> s h c", c=NOPE),
-                        )
-                        nc.sync.dma_start(
-                            out=out[b, :, head0 : head0 + heads, :], in_=result[b][:, head0 : head0 + heads, :]
-                        )

@@ -23,8 +23,9 @@ PASSES = DIM // K_PASS
 BANK = 512
 ROTARY_COL0 = HEADS * NOPE
 ROTARY_ROUNDS = HEADS * ROPE // BANK
-ROUNDS = HEADS * QK // BANK
-UNITS = ROUNDS * PASSES
+PLAIN_ROUNDS = ((0, BANK), (BANK, BANK), (2 * BANK, BANK), (3 * BANK, BANK // 2), (3 * BANK + BANK // 2, BANK // 2))
+WIDTHS = (BANK,) * ROTARY_ROUNDS + tuple(width for first, width in PLAIN_ROUNDS)
+UNITS = len(WIDTHS) * PASSES
 ROTARY_BANKS = ROTARY_ROUNDS * BATCH
 VECTOR_COLS = 320
 FLOPS = 2 * BATCH * P * DIM * HEADS * QK
@@ -34,7 +35,7 @@ def tile_mla_pa_kernel(tc, x, w, freqs, out):
     nc = tc.nc
     with tc.tile_pool(name="const", bufs=1) as const, tc.tile_pool(name="keep", bufs=1) as keep, tc.tile_pool(
         name="x_in", bufs=BATCH
-    ) as x_in, tc.tile_pool(name="x_side", bufs=2) as x_side, tc.tile_pool(
+    ) as x_in, tc.tile_pool(name="x_side", bufs=BATCH) as x_side, tc.tile_pool(
         name="w_narrow", bufs=ROTARY_ROUNDS * PASSES
     ) as w_narrow, tc.tile_pool(name="w_wide", bufs=2 * PASSES) as w_wide, tc.tile_pool(
         name="w_side", bufs=4
@@ -43,11 +44,11 @@ def tile_mla_pa_kernel(tc, x, w, freqs, out):
     ) as psum, tc.manual_schedule():
         angles = const.tile([P, PAIRS], BF16)
         nc.scalar.dma_start(out=angles[:], in_=freqs)
-        x_rows = []
-        for b in range(BATCH):
+
+        def load_x(b):
             rows = x_in.tile([P, DIM], BF16, name="x_rows")
             nc.sync.dma_start(out=rows[:], in_=x[b])
-            x_rows.append(rows)
+            return rows
 
         def load_w(pool, col0, width, g):
             rows = pool.tile([P, PACK, width], BF16, name="w_rows")
@@ -57,13 +58,19 @@ def tile_mla_pa_kernel(tc, x, w, freqs, out):
             )
             return rows
 
-        w_rows = []
-        for r in range(ROTARY_ROUNDS):
+        first_round = [load_w(w_narrow, ROTARY_COL0, BANK, 0)[:]]
+        x_rows = [load_x(0)]
+        first_round.append(load_w(w_narrow, ROTARY_COL0, BANK, 1)[:])
+        x_rows.extend([load_x(b) for b in range(1, BATCH)])
+        first_round.extend([load_w(w_narrow, ROTARY_COL0, BANK, g)[:] for g in range(2, PASSES)])
+        w_rows = [first_round]
+        for r in range(1, ROTARY_ROUNDS):
             w_rows.append([load_w(w_narrow, ROTARY_COL0 + r * BANK, BANK, g)[:] for g in range(PASSES)])
         for col0 in range(0, ROTARY_COL0, 2 * BANK):
             wide = [load_w(w_wide, col0, 2 * BANK, g) for g in range(PASSES)]
-            for half in range(2):
-                w_rows.append([rows[:, :, half * BANK : (half + 1) * BANK] for rows in wide])
+            for first, width in PLAIN_ROUNDS:
+                if col0 <= first < col0 + 2 * BANK:
+                    w_rows.append([rows[:, :, first - col0 : first - col0 + width] for rows in wide])
 
         sines = const.tile([P, 2, PAIRS], F32)
         nc.scalar.activation(out=sines[:, 0, :], in_=angles[:], func=ACT.Sin, scale=-1.0)
@@ -75,38 +82,37 @@ def tile_mla_pa_kernel(tc, x, w, freqs, out):
         make_identity(nc, ident[:])
         x_codes = keep.tile([P, BATCH, PASSES * P], U32, align_bytes=64)
         x_scales = keep.tile([P, BATCH, PASSES * P], U8, align_bytes=64)
-        for b in range(BATCH):
+        result = [keep.tile([P, HEADS, QK], F32, name="result%d" % b) for b in range(BATCH)]
+
+        def flip_x(b):
             x_words = x_rows[b][:].bitcast(F32).rearrange("s (g q u) -> s g u q", g=PASSES, u=2)
-            x_grouped = x_side.tile([P, PASSES * P * PACK], BF16, align_bytes=64)
-            grouped_words = x_grouped[:].bitcast(F32).rearrange("q (g s u) -> q g s u", g=PASSES, u=2)
+            flipped_banks = []
             for first in range(0, PASSES, 2):
                 flipped = psum.tile([P, 2, 2, P], F32, tag="bank")
                 for i in range(2):
                     for u in range(2):
                         nc.tensor.transpose(flipped[:, i, u, :], x_words[:, first + i, u, :], ident[:])
+                flipped_banks.append(flipped)
+            return flipped_banks
+
+        def lay_x(flipped_banks):
+            x_grouped = x_side.tile([P, PASSES * P * PACK], BF16, align_bytes=64)
+            grouped_words = x_grouped[:].bitcast(F32).rearrange("q (g s u) -> q g s u", g=PASSES, u=2)
+            for n, flipped in enumerate(flipped_banks):
                 nc.scalar.copy(
-                    out=grouped_words[:, first : first + 2, :, :], in_=flipped[:].rearrange("q g u s -> q g s u")
+                    out=grouped_words[:, 2 * n : 2 * n + 2, :, :], in_=flipped[:].rearrange("q g u s -> q g s u")
                 )
+            return x_grouped
+
+        def quantise_x(b, x_grouped):
             nc.vector.quantize_mx(out=x_codes[:, b, :].bitcast(FP8X4), scales=x_scales[:, b, :], in_=x_grouped[:])
 
-        sin_half_sq = const.tile([P, PAIRS], F32)
-        nc.vector.tensor_tensor(out=sin_half_sq[:], in0=sin_half[:], in1=sin_half[:], op=ALU.mult)
-        cosines = const.tile([P, PAIRS, 2], F32)
-        nc.vector.tensor_scalar(
-            out=cosines[:],
-            in0=sin_half_sq[:].unsqueeze(2).to_broadcast([P, PAIRS, 2]),
-            scalar1=-2.0,
-            scalar2=1.0,
-            op0=ALU.mult,
-            op1=ALU.add,
-        )
-
-        result = [keep.tile([P, HEADS, QK], F32, name="result%d" % b) for b in range(BATCH)]
-
-        def regroup(unit, vector_cols):
+        def regroup(unit, vector_share):
             rows = w_rows[unit // PASSES][unit % PASSES]
-            w_grouped = w_side.tile([P, BANK, PACK], BF16, align_bytes=64)
-            for copy, lo, hi in ((nc.vector.tensor_copy, 0, vector_cols), (nc.scalar.copy, vector_cols, BANK)):
+            width = WIDTHS[unit // PASSES]
+            vector_cols = width * vector_share // BANK
+            w_grouped = w_side.tile([P, width, PACK], BF16, align_bytes=64, name="w_grouped")
+            for copy, lo, hi in ((nc.vector.tensor_copy, 0, vector_cols), (nc.scalar.copy, vector_cols, width)):
                 if lo < hi:
                     copy(
                         out=w_grouped[:, lo:hi, :].rearrange("p (c i) j -> p c j i", i=4),
@@ -114,13 +120,17 @@ def tile_mla_pa_kernel(tc, x, w, freqs, out):
                     )
             return w_grouped
 
-        def multiply(unit, w_grouped, banks):
-            g = unit % PASSES
-            w_codes = w_mx.tile([P, BANK], U32, align_bytes=64)
-            w_scales = w_mx.tile([P, BANK], U8, align_bytes=64)
+        def quantise(unit, w_grouped):
+            width = WIDTHS[unit // PASSES]
+            w_codes = w_mx.tile([P, width], U32, align_bytes=64, name="w_codes")
+            w_scales = w_mx.tile([P, width], U8, align_bytes=64, name="w_scales")
             nc.vector.quantize_mx(
                 out=w_codes[:].bitcast(FP8X4), scales=w_scales[:], in_=w_grouped[:].rearrange("p n j -> p (n j)")
             )
+            return w_codes, w_scales
+
+        def multiply(unit, w_codes, w_scales, banks):
+            g = unit % PASSES
             for b in range(BATCH):
                 nc.tensor.matmul_mx(
                     out=banks[b][:],
@@ -161,24 +171,55 @@ def tile_mla_pa_kernel(tc, x, w, freqs, out):
             nc.vector.tensor_tensor(out=pairs, in0=pairs, in1=crossed[:].rearrange("s e h j -> s h j e"), op=ALU.add)
 
         def store_plain(n, bank, copy):
-            heads = BANK // NOPE
-            head0 = (n // BATCH) * heads
+            first, width = PLAIN_ROUNDS[n // BATCH]
+            heads = width // NOPE
+            head0 = first // NOPE
             b = n % BATCH
             copy(out=result[b][:, head0 : head0 + heads, 0:NOPE], in_=bank[:].rearrange("s (h c) -> s h c", c=NOPE))
             nc.sync.dma_start(out=out[b, :, head0 : head0 + heads, :], in_=result[b][:, head0 : head0 + heads, :])
 
+        regrouped = [regroup(0, VECTOR_COLS)]
+        flipped_x = [flip_x(0)]
+        quantised = [quantise(0, regrouped[0])]
+        sin_half_sq = const.tile([P, PAIRS], F32)
+        nc.vector.tensor_tensor(out=sin_half_sq[:], in0=sin_half[:], in1=sin_half[:], op=ALU.mult)
+        cosines = const.tile([P, PAIRS, 2], F32)
+        nc.vector.tensor_scalar(
+            out=cosines[:],
+            in0=sin_half_sq[:].unsqueeze(2).to_broadcast([P, PAIRS, 2]),
+            scalar1=-2.0,
+            scalar2=1.0,
+            op0=ALU.mult,
+            op1=ALU.add,
+        )
+        x_grouped = [lay_x(flipped_x[0])]
+        regrouped.append(regroup(1, VECTOR_COLS))
+        flipped_x.append(flip_x(1))
+        quantise_x(0, x_grouped[0])
+        quantised.append(quantise(1, regrouped[1]))
+        for b in range(1, BATCH):
+            x_grouped.append(lay_x(flipped_x[b]))
+            if b + 1 < BATCH:
+                flipped_x.append(flip_x(b + 1))
+            else:
+                regrouped.append(regroup(2, VECTOR_COLS))
+            quantise_x(b, x_grouped[b])
+        HEAD_UNITS = 2
+
         banks = []
         side_tiles = []
-        regrouped = [regroup(0, VECTOR_COLS)]
         for step in range(UNITS + BATCH):
             emptied = step - PASSES
             rotating = 0 <= emptied < ROTARY_BANKS
-            if step + 1 < UNITS:
+            if HEAD_UNITS <= step and step + 1 < UNITS:
                 regrouped.append(regroup(step + 1, 0 if rotating else VECTOR_COLS))
             if step < UNITS:
                 if step % PASSES == 0:
-                    banks.extend(psum.tile([P, BANK], F32, tag="bank", name="bank%d" % b) for b in range(BATCH))
-                multiply(step, regrouped[step], banks[-BATCH:])
+                    width = WIDTHS[step // PASSES]
+                    banks.extend([psum.tile([P, width], F32, tag="bank", name="bank%d" % b) for b in range(BATCH)])
+                if HEAD_UNITS <= step:
+                    quantised.append(quantise(step, regrouped[step]))
+                multiply(step, quantised[step][0], quantised[step][1], banks[-BATCH:])
             if rotating:
                 side_tiles.append(rotation_products(emptied, banks[emptied]))
             if 0 <= emptied - 1 < ROTARY_BANKS:

@@ -28,6 +28,7 @@ WIDTHS = (BANK,) * ROTARY_ROUNDS + tuple(width for first, width in PLAIN_ROUNDS)
 UNITS = len(WIDTHS) * PASSES
 ROTARY_BANKS = ROTARY_ROUNDS * BATCH
 VECTOR_COLS = 320
+LIGHT_VECTOR_COLS = 416
 FLOPS = 2 * BATCH * P * DIM * HEADS * QK
 
 
@@ -38,7 +39,7 @@ def tile_mla_pa_kernel(tc, x, w, freqs, out):
     ) as x_in, tc.tile_pool(name="x_side", bufs=BATCH) as x_side, tc.tile_pool(
         name="w_narrow", bufs=ROTARY_ROUNDS * PASSES
     ) as w_narrow, tc.tile_pool(name="w_wide", bufs=2 * PASSES) as w_wide, tc.tile_pool(
-        name="w_side", bufs=4
+        name="w_side", bufs=6
     ) as w_side, tc.tile_pool(name="w_mx", bufs=4) as w_mx, tc.tile_pool(name="turn", bufs=3) as turn, tc.psum_pool(
         name="psum", bufs=8
     ) as psum, tc.manual_schedule():
@@ -72,9 +73,9 @@ def tile_mla_pa_kernel(tc, x, w, freqs, out):
                 if col0 <= first < col0 + 2 * BANK:
                     w_rows.append([rows[:, :, first - col0 : first - col0 + width] for rows in wide])
 
-        sines = const.tile([P, 2, PAIRS], F32)
-        nc.scalar.activation(out=sines[:, 0, :], in_=angles[:], func=ACT.Sin, scale=-1.0)
-        nc.scalar.activation(out=sines[:, 1, :], in_=angles[:], func=ACT.Sin)
+        sines = const.tile([P, PAIRS, 2], F32)
+        nc.scalar.activation(out=sines[:, :, 0], in_=angles[:], func=ACT.Sin, scale=-1.0)
+        nc.scalar.activation(out=sines[:, :, 1], in_=angles[:], func=ACT.Sin)
         sin_half = const.tile([P, PAIRS], F32)
         nc.scalar.activation(out=sin_half[:], in_=angles[:], func=ACT.Sin, scale=0.5)
 
@@ -156,19 +157,19 @@ def tile_mla_pa_kernel(tc, x, w, freqs, out):
                 op=ALU.mult,
             )
             pairs = bank[:].rearrange("s (h j e) -> s h j e", j=PAIRS, e=2)
-            crossed = turn.tile([P, 2, heads, PAIRS], F32)
-            for e in range(2):
-                nc.vector.tensor_tensor(
-                    out=crossed[:, e, :, :],
-                    in0=pairs[:, :, :, 1 - e],
-                    in1=sines[:, e, :].unsqueeze(1).to_broadcast([P, heads, PAIRS]),
-                    op=ALU.mult,
-                )
+            crossed = turn.tile([P, heads, PAIRS, 2], F32)
+            nc.vector.tensor_tensor(
+                out=crossed[:],
+                in0=pairs[:, :, :, ::-1],
+                in1=sines[:].unsqueeze(1).to_broadcast([P, heads, PAIRS, 2]),
+                op=ALU.mult,
+            )
             return crossed
 
         def rotation_sum(n, crossed):
-            pairs = rotary_part(n).rearrange("s h (j e) -> s h j e", e=2)
-            nc.vector.tensor_tensor(out=pairs, in0=pairs, in1=crossed[:].rearrange("s e h j -> s h j e"), op=ALU.add)
+            nc.vector.tensor_tensor(
+                out=rotary_part(n), in0=rotary_part(n), in1=crossed[:].rearrange("s h j e -> s h (j e)"), op=ALU.add
+            )
 
         def store_plain(n, bank, copy):
             first, width = PLAIN_ROUNDS[n // BATCH]
@@ -204,15 +205,19 @@ def tile_mla_pa_kernel(tc, x, w, freqs, out):
             else:
                 regrouped.append(regroup(2, VECTOR_COLS))
             quantise_x(b, x_grouped[b])
+        regrouped.append(regroup(3, VECTOR_COLS))
         HEAD_UNITS = 2
+        AHEAD = 2
 
         banks = []
         side_tiles = []
         for step in range(UNITS + BATCH):
             emptied = step - PASSES
             rotating = 0 <= emptied < ROTARY_BANKS
-            if HEAD_UNITS <= step and step + 1 < UNITS:
-                regrouped.append(regroup(step + 1, 0 if rotating else VECTOR_COLS))
+            if HEAD_UNITS <= step and step + AHEAD < UNITS:
+                light_vector = emptied >= 0 and WIDTHS[step // PASSES] < WIDTHS[emptied // BATCH]
+                share = 0 if rotating else LIGHT_VECTOR_COLS if light_vector else VECTOR_COLS
+                regrouped.append(regroup(step + AHEAD, share))
             if step < UNITS:
                 if step % PASSES == 0:
                     width = WIDTHS[step // PASSES]

@@ -116,8 +116,8 @@ def tile_mla_pa_kernel(tc, x, w, freqs, out):
             for copy, lo, hi in ((nc.vector.tensor_copy, 0, vector_cols), (nc.scalar.copy, vector_cols, width)):
                 if lo < hi:
                     copy(
-                        out=w_grouped[:, lo:hi, :].rearrange("p (c i) j -> p c j i", i=4),
-                        in_=rows[:, :, lo:hi].rearrange("p j (c i) -> p c j i", i=4),
+                        out=w_grouped[:, lo:hi, :].rearrange("p (c i) j -> p c j i", i=8),
+                        in_=rows[:, :, lo:hi].rearrange("p j (c i) -> p c j i", i=8),
                     )
             return w_grouped
 

import concourse.mybir as mybir
from concourse.masks import make_identity

BF16 = mybir.dt.bfloat16
F32 = mybir.dt.float32
U32 = mybir.dt.uint32
U8 = mybir.dt.uint8
FP8X4 = mybir.dt.float8_e4m3fn_x4
ACT = mybir.ActivationFunctionType
ALU = mybir.AluOpType

P = 128
PACK = 4
K_PASS = P * PACK
BATCH = 4
DIM = 2048
HEADS = 16
NOPE = 128
ROPE = 64
QK = NOPE + ROPE
PAIRS = ROPE // 2
PASSES = DIM // K_PASS
BANK = 512
ROTARY_COL0 = HEADS * NOPE
ROTARY_ROUNDS = HEADS * ROPE // BANK
PLAIN_ROUNDS = ((0, BANK), (BANK, BANK), (2 * BANK, BANK), (3 * BANK, BANK // 2), (3 * BANK + BANK // 2, BANK // 2))
WIDTHS = (BANK,) * ROTARY_ROUNDS + tuple(width for first, width in PLAIN_ROUNDS)
UNITS = len(WIDTHS) * PASSES
ROTARY_BANKS = ROTARY_ROUNDS * BATCH
VECTOR_COLS = 320
LIGHT_VECTOR_COLS = 416
FLOPS = 2 * BATCH * P * DIM * HEADS * QK


def tile_mla_pa_kernel(tc, x, w, freqs, out):
    nc = tc.nc
    with tc.tile_pool(name="const", bufs=1) as const, tc.tile_pool(name="keep", bufs=1) as keep, tc.tile_pool(
        name="x_in", bufs=BATCH
    ) as x_in, tc.tile_pool(name="x_side", bufs=BATCH) as x_side, tc.tile_pool(
        name="w_narrow", bufs=ROTARY_ROUNDS * PASSES
    ) as w_narrow, tc.tile_pool(name="w_wide", bufs=2 * PASSES) as w_wide, tc.tile_pool(
        name="w_side", bufs=6
    ) as w_side, tc.tile_pool(name="w_mx", bufs=4) as w_mx, tc.tile_pool(name="turn", bufs=3) as turn, tc.psum_pool(
        name="psum", bufs=8
    ) as psum, tc.manual_schedule():
        angles = const.tile([P, PAIRS], BF16)
        nc.scalar.dma_start(out=angles[:], in_=freqs)

        def load_x(b):
            rows = x_in.tile([P, DIM], BF16, name="x_rows")
            nc.sync.dma_start(out=rows[:], in_=x[b])
            return rows

        def load_w(pool, col0, width, g):
            rows = pool.tile([P, PACK, width], BF16, name="w_rows")
            nc.sync.dma_start(
                out=rows[:],
                in_=w[g * K_PASS : (g + 1) * K_PASS, col0 : col0 + width].rearrange("(p j) n -> p j n", j=PACK),
            )
            return rows

        first_round = [load_w(w_narrow, ROTARY_COL0, BANK, 0)[:]]
        x_rows = [load_x(0)]
        first_round.append(load_w(w_narrow, ROTARY_COL0, BANK, 1)[:])
        x_rows.extend([load_x(b) for b in range(1, BATCH)])
        first_round.extend([load_w(w_narrow, ROTARY_COL0, BANK, g)[:] for g in range(2, PASSES)])
        w_rows = [first_round]
        for r in range(1, ROTARY_ROUNDS):
            w_rows.append([load_w(w_narrow, ROTARY_COL0 + r * BANK, BANK, g)[:] for g in range(PASSES)])
        for col0 in range(0, ROTARY_COL0, 2 * BANK):
            wide = [load_w(w_wide, col0, 2 * BANK, g) for g in range(PASSES)]
            for first, width in PLAIN_ROUNDS:
                if col0 <= first < col0 + 2 * BANK:
                    w_rows.append([rows[:, :, first - col0 : first - col0 + width] for rows in wide])

        sines = const.tile([P, PAIRS, 2], F32)
        nc.scalar.activation(out=sines[:, :, 0], in_=angles[:], func=ACT.Sin, scale=-1.0)
        nc.scalar.activation(out=sines[:, :, 1], in_=angles[:], func=ACT.Sin)
        sin_half = const.tile([P, PAIRS], F32)
        nc.scalar.activation(out=sin_half[:], in_=angles[:], func=ACT.Sin, scale=0.5)

        ident = const.tile([P, P], F32)
        make_identity(nc, ident[:])
        x_codes = keep.tile([P, BATCH, PASSES * P], U32, align_bytes=64)
        x_scales = keep.tile([P, BATCH, PASSES * P], U8, align_bytes=64)
        result = [keep.tile([P, HEADS, QK], F32, name="result%d" % b) for b in range(BATCH)]

        def flip_x(b):
            x_words = x_rows[b][:].bitcast(F32).rearrange("s (g q u) -> s g u q", g=PASSES, u=2)
            flipped_banks = []
            for first in range(0, PASSES, 2):
                flipped = psum.tile([P, 2, 2, P], F32, tag="bank")
                for i in range(2):
                    for u in range(2):
                        nc.tensor.transpose(flipped[:, i, u, :], x_words[:, first + i, u, :], ident[:])
                flipped_banks.append(flipped)
            return flipped_banks

        def lay_x(flipped_banks):
            x_grouped = x_side.tile([P, PASSES * P * PACK], BF16, align_bytes=64)
            grouped_words = x_grouped[:].bitcast(F32).rearrange("q (g s u) -> q g s u", g=PASSES, u=2)
            for n, flipped in enumerate(flipped_banks):
                nc.scalar.copy(
                    out=grouped_words[:, 2 * n : 2 * n + 2, :, :], in_=flipped[:].rearrange("q g u s -> q g s u")
                )
            return x_grouped

        def quantise_x(b, x_grouped):
            nc.vector.quantize_mx(out=x_codes[:, b, :].bitcast(FP8X4), scales=x_scales[:, b, :], in_=x_grouped[:])

        def regroup(unit, vector_share):
            rows = w_rows[unit // PASSES][unit % PASSES]
            width = WIDTHS[unit // PASSES]
            vector_cols = width * vector_share // BANK
            w_grouped = w_side.tile([P, width, PACK], BF16, align_bytes=64, name="w_grouped")
            for copy, lo, hi in ((nc.vector.tensor_copy, 0, vector_cols), (nc.scalar.copy, vector_cols, width)):
                if lo < hi:
                    copy(
                        out=w_grouped[:, lo:hi, :].rearrange("p (c i) j -> p c j i", i=8),
                        in_=rows[:, :, lo:hi].rearrange("p j (c i) -> p c j i", i=8),
                    )
            return w_grouped

        def quantise(unit, w_grouped):
            width = WIDTHS[unit // PASSES]
            w_codes = w_mx.tile([P, width], U32, align_bytes=64, name="w_codes")
            w_scales = w_mx.tile([P, width], U8, align_bytes=64, name="w_scales")
            nc.vector.quantize_mx(
                out=w_codes[:].bitcast(FP8X4), scales=w_scales[:], in_=w_grouped[:].rearrange("p n j -> p (n j)")
            )
            return w_codes, w_scales

        def multiply(unit, w_codes, w_scales, banks):
            g = unit % PASSES
            for b in range(BATCH):
                nc.tensor.matmul_mx(
                    out=banks[b][:],
                    lhsT=x_codes[:, b, g * P : (g + 1) * P].bitcast(FP8X4),
                    lhsT_scale=x_scales[:, b, g * P : (g + 1) * P],
                    rhs=w_codes[:].bitcast(FP8X4),
                    rhs_scale=w_scales[:],
                    start=(g == 0),
                    stop=(g == PASSES - 1),
                )

        def rotary_part(n):
            heads = BANK // ROPE
            head0 = (n // BATCH) * heads
            return result[n % BATCH][:, head0 : head0 + heads, NOPE:QK]

        def rotation_products(n, bank):
            heads = BANK // ROPE
            nc.vector.tensor_tensor(
                out=rotary_part(n),
                in0=bank[:].rearrange("s (h c) -> s h c", c=ROPE),
                in1=cosines[:].rearrange("s j e -> s (j e)").unsqueeze(1).to_broadcast([P, heads, ROPE]),
                op=ALU.mult,
            )
            pairs = bank[:].rearrange("s (h j e) -> s h j e", j=PAIRS, e=2)
            crossed = turn.tile([P, heads, PAIRS, 2], F32)
            nc.vector.tensor_tensor(
                out=crossed[:],
                in0=pairs[:, :, :, ::-1],
                in1=sines[:].unsqueeze(1).to_broadcast([P, heads, PAIRS, 2]),
                op=ALU.mult,
            )
            return crossed

        def rotation_sum(n, crossed):
            nc.vector.tensor_tensor(
                out=rotary_part(n), in0=rotary_part(n), in1=crossed[:].rearrange("s h j e -> s h (j e)"), op=ALU.add
            )

        def store_plain(n, bank, copy):
            first, width = PLAIN_ROUNDS[n // BATCH]
            heads = width // NOPE
            head0 = first // NOPE
            b = n % BATCH
            copy(out=result[b][:, head0 : head0 + heads, 0:NOPE], in_=bank[:].rearrange("s (h c) -> s h c", c=NOPE))
            nc.sync.dma_start(out=out[b, :, head0 : head0 + heads, :], in_=result[b][:, head0 : head0 + heads, :])

        regrouped = [regroup(0, VECTOR_COLS)]
        flipped_x = [flip_x(0)]
        quantised = [quantise(0, regrouped[0])]
        sin_half_sq = const.tile([P, PAIRS], F32)
        nc.vector.tensor_tensor(out=sin_half_sq[:], in0=sin_half[:], in1=sin_half[:], op=ALU.mult)
        cosines = const.tile([P, PAIRS, 2], F32)
        nc.vector.tensor_scalar(
            out=cosines[:],
            in0=sin_half_sq[:].unsqueeze(2).to_broadcast([P, PAIRS, 2]),
            scalar1=-2.0,
            scalar2=1.0,
            op0=ALU.mult,
            op1=ALU.add,
        )
        x_grouped = [lay_x(flipped_x[0])]
        regrouped.append(regroup(1, VECTOR_COLS))
        flipped_x.append(flip_x(1))
        quantise_x(0, x_grouped[0])
        quantised.append(quantise(1, regrouped[1]))
        for b in range(1, BATCH):
            x_grouped.append(lay_x(flipped_x[b]))
            if b + 1 < BATCH:
                flipped_x.append(flip_x(b + 1))
            else:
                regrouped.append(regroup(2, VECTOR_COLS))
            quantise_x(b, x_grouped[b])
        regrouped.append(regroup(3, VECTOR_COLS))
        HEAD_UNITS = 2
        AHEAD = 2

        banks = []
        side_tiles = []
        for step in range(UNITS + BATCH):
            emptied = step - PASSES
            rotating = 0 <= emptied < ROTARY_BANKS
            if HEAD_UNITS <= step and step + AHEAD < UNITS:
                light_vector = emptied >= 0 and WIDTHS[step // PASSES] < WIDTHS[emptied // BATCH]
                share = 0 if rotating else LIGHT_VECTOR_COLS if light_vector else VECTOR_COLS
                regrouped.append(regroup(step + AHEAD, share))
            if step < UNITS:
                if step % PASSES == 0:
                    width = WIDTHS[step // PASSES]
                    banks.extend([psum.tile([P, width], F32, tag="bank", name="bank%d" % b) for b in range(BATCH)])
                if HEAD_UNITS <= step:
                    quantised.append(quantise(step, regrouped[step]))
                multiply(step, quantised[step][0], quantised[step][1], banks[-BATCH:])
            if rotating:
                side_tiles.append(rotation_products(emptied, banks[emptied]))
            if 0 <= emptied - 1 < ROTARY_BANKS:
                rotation_sum(emptied - 1, side_tiles[emptied - 1])
            if emptied >= ROTARY_BANKS:
                idle_vector = step >= UNITS and emptied % 2 == 1
                store_plain(
                    emptied - ROTARY_BANKS, banks[emptied], nc.vector.tensor_copy if idle_vector else nc.scalar.copy
                )
